import numpy as np
import ml_dtypes


def mxq(x, axis, fmt="e4m3"):
    dtype, down = {"e4m3": (ml_dtypes.float8_e4m3fn, 7), "e5m2": (ml_dtypes.float8_e5m2, 14)}[fmt]
    v = np.moveaxis(np.asarray(x, np.float32).astype(ml_dtypes.bfloat16).astype(np.float64), axis, -1)
    blocks = v.reshape(v.shape[:-1] + (-1, 32))
    amax = np.abs(blocks).max(-1, keepdims=True)
    byte = np.maximum(np.where(amax > 0, np.frexp(amax)[1] - 1 + 127, 0) - down, 1)
    scale = np.exp2(byte - 127.0)
    codes = (blocks / scale).astype(np.float32).astype(dtype).astype(np.float64)
    return np.moveaxis((codes * scale).reshape(v.shape), -1, axis)


WIDE = False


def mx_kscale(k):
    if not WIDE:
        return np.ones(k)
    levels = np.array([10, -10, 5, -5, 0])
    a = np.random.permutation(np.resize(levels, k // 512 * 4)).reshape(k // 512, 4)
    idx = np.arange(k)
    return np.exp2(a[idx // 512, idx % 128 // 32])


BF16 = ml_dtypes.bfloat16


def bf(x):
    return np.asarray(x, np.float32).astype(BF16)


def f64(x):
    return np.asarray(x).astype(np.float64)


E2M1 = np.array([0.0, 0.5, 1.0, 1.5, 2.0, 3.0, 4.0, 6.0, -0.0, -0.5, -1.0, -1.5, -2.0, -3.0, -4.0, -6.0])


def pack_weight(w, fmt):
    k, n = w.shape
    w = f64(bf(w)).reshape(k // 32, 32, n)
    amax = np.abs(w).max(1)
    if fmt == "e4m3":
        byte = np.frexp(amax)[1] - 1 + 127 - 7
    else:
        mant, ex = np.frexp(amax / 6.0)
        byte = np.where(mant > 0.5, ex, ex - 1) + 127
    byte = np.clip(np.where(amax > 0, byte, 1), 1, 254)
    scaled = (w * np.exp2(127.0 - byte)[:, None, :]).reshape(k, n).astype(np.float32)
    by_word = np.ascontiguousarray(scaled.reshape(k // 512, 128, 4, n).transpose(0, 1, 3, 2))
    if fmt == "e4m3":
        words = by_word.astype(ml_dtypes.float8_e4m3fn).view(np.uint8)
    else:
        c = by_word.astype(ml_dtypes.float4_e2m1fn).view(np.uint8) & 0xF
        words = c[..., 0::2] | (c[..., 1::2] << 4)
    return np.ascontiguousarray(words), np.ascontiguousarray(byte.astype(np.uint8).reshape(k // 512, 16, n))


def unpack_weight(words, scales, fmt):
    g, p, n, _ = words.shape
    if fmt == "e4m3":
        vals = np.ascontiguousarray(words).view(ml_dtypes.float8_e4m3fn).astype(np.float64)
    else:
        nib = np.empty((g, p, n, 4), np.uint8)
        nib[..., 0::2] = words & 0xF
        nib[..., 1::2] = words >> 4
        vals = E2M1[nib]
    vals = vals * np.repeat(np.exp2(scales.astype(np.float64) - 127.0), 8, axis=1)[..., None]
    return vals.transpose(0, 1, 3, 2).reshape(g * 512, n)


M, D, F = 512, 1024, 3584


def silu(v):
    return v / (1.0 + np.exp(-v))


def setup_inputs():
    s, t = mx_kscale(D), mx_kscale(F)
    x = np.random.standard_normal((M, D)) * s
    wg = np.random.standard_normal((D, F)) * 0.04 / s[:, None]
    wu = np.random.standard_normal((D, F)) * 0.04 / s[:, None] * t
    wd = np.random.standard_normal((F, D)) * 0.02 / t[:, None]
    gate_words, gate_scales = pack_weight(wg, "e4m3")
    up_words, up_scales = pack_weight(wu, "e4m3")
    down_words, down_scales = pack_weight(wd, "e4m3")
    return {"x": bf(x), "gate_words": gate_words, "gate_scales": gate_scales, "up_words": up_words, "up_scales": up_scales,
            "down_words": down_words, "down_scales": down_scales}


def reference(x, gate_words, gate_scales, up_words, up_scales, down_words, down_scales):
    wg = unpack_weight(gate_words, gate_scales, "e4m3")
    wu = unpack_weight(up_words, up_scales, "e4m3")
    wd = unpack_weight(down_words, down_scales, "e4m3")
    xq = mxq(f64(x), 1, "e4m3")
    gate = xq @ wg
    up = xq @ wu
    h = silu(gate) * up
    return mxq(h, 1, "e4m3") @ wd

@@ -1,0 +1,195 @@
+from contextlib import ExitStack
+
+import concourse.mybir as mybir
+from concourse.masks import make_identity
+
+F32 = mybir.dt.float32
+BF16 = mybir.dt.bfloat16
+I32 = mybir.dt.int32
+U32 = mybir.dt.uint32
+U8 = mybir.dt.uint8
+FP8X4 = mybir.dt.float8_e4m3fn_x4
+SILU = mybir.ActivationFunctionType.Silu
+MULT = mybir.AluOpType.mult
+
+P = 128
+M, D, F = 512, 1024, 3584
+N = 512
+TOK = M // P
+KX = D // 512
+KH = F // 512
+DC = D // N
+
+FLOPS = 2 * M * D * F * 3
+
+
+def tile_nvfp4persistentmlp_kernel(
+    tc, x, gate_words, gate_scales, up_words, up_scales, down_words, down_scales, out
+):
+    nc = tc.nc
+    with ExitStack() as ctx:
+        keep = ctx.enter_context(tc.tile_pool(name="keep", bufs=1))
+        work = ctx.enter_context(tc.tile_pool(name="work", bufs=1))
+        psum = ctx.enter_context(tc.psum_pool(name="psum", bufs=1))
+        ctx.enter_context(tc.manual_schedule())
+
+        def bank(b, shape, dtype, name):
+            return psum.tile(shape, dtype, name=name, tag="bank%d" % b)
+
+        s1 = keep.tile([P, F], U8, name="s1", align_bytes=64)
+        s2 = keep.tile([P, 2, D], U8, name="s2", align_bytes=64)
+        warm = keep.tile([P, 1], F32, name="warm")
+        warm2 = keep.tile([P, 1], F32, name="warm2")
+        nc.vector.memset(s1[:].bitcast(I32), 0)
+        nc.vector.memset(warm[:], 0.0)
+        nc.vector.memset(s2[:].bitcast(I32), 0)
+        nc.scalar.activation(out=warm2[:], in_=warm[:], func=SILU)
+        ident_f = keep.tile([P, P], F32, name="ident_f")
+        ident_b = keep.tile([P, P], BF16, name="ident_b")
+        make_identity(nc, ident_f[:])
+        make_identity(nc, ident_b[:])
+
+        x_sb = [keep.tile([P, D], BF16, name="x%d" % i) for i in range(TOK)]
+        gw = [keep.tile([P, KX, N], U32, name="gw%d" % g, align_bytes=64) for g in range(KH)]
+        uw = [keep.tile([P, KX, N], U32, name="uw%d" % g, align_bytes=64) for g in range(KH)]
+        dw = [keep.tile([P, D], U32, name="dw%d" % g, align_bytes=64) for g in range(KH)]
+        gate_i32 = gate_words.rearrange("g p n t -> p g (n t)").bitcast(I32)
+        up_i32 = up_words.rearrange("g p n t -> p g (n t)").bitcast(I32)
+        s1_i32 = s1[:].bitcast(I32)
+        s2_i32 = s2[:].bitcast(I32)
+        gs_i32 = gate_scales.bitcast(I32)
+        us_i32 = up_scales.bitcast(I32)
+        ds_i32 = down_scales.bitcast(I32)
+
+        def load_stage1_words(dst, src, g):
+            nc.sync.dma_start(out=dst[g][:].bitcast(I32), in_=src[:, :, N * g : N * (g + 1)])
+
+        for i in range(TOK):
+            nc.sync.dma_start(out=x_sb[i][:], in_=x[P * i : P * (i + 1), :])
+        load_stage1_words(gw, gate_i32, 0)
+        for q in range(4):
+            nc.sync.dma_start(out=s1_i32[32 * q : 32 * q + 8, :], in_=gs_i32[:, 4 * q : 4 * q + 4, :])
+        load_stage1_words(uw, up_i32, 0)
+        for q in range(4):
+            nc.sync.dma_start(out=s1_i32[32 * q + 8 : 32 * q + 16, :], in_=us_i32[:, 4 * q : 4 * q + 4, :])
+        for g in range(1, KH):
+            load_stage1_words(gw, gate_i32, g)
+            load_stage1_words(uw, up_i32, g)
+        for g in range(KH):
+            nc.sync.dma_start(
+                out=dw[g][:].bitcast(I32), in_=down_words[g].rearrange("p n t -> p (n t)").bitcast(I32)
+            )
+        for q in range(4):
+            nc.sync.dma_start(out=s2_i32[32 * q : 32 * q + 16, 0, :], in_=ds_i32[0:4, 4 * q : 4 * q + 4, :])
+        for q in range(4):
+            nc.sync.dma_start(out=s2_i32[32 * q : 32 * q + 12, 1, :], in_=ds_i32[4:7, 4 * q : 4 * q + 4, :])
+
+        xq = [keep.tile([P, KX * P], U32, name="xq%d" % i, align_bytes=64) for i in range(TOK)]
+        xs = [keep.tile([P, KX * P], U8, name="xs%d" % i, align_bytes=64) for i in range(TOK)]
+        xg = [keep.tile([P, KX * P * 4], BF16, name="xg%d" % i, align_bytes=64) for i in range(TOK)]
+        for i in range(TOK):
+            x_words = x_sb[i][:].bitcast(F32)
+            xg_words = xg[i][:].bitcast(F32)
+            for kg in range(KX):
+                xt = bank(2 * i + kg, [P, 2, P], F32, "xt")
+                for u in range(2):
+                    nc.tensor.transpose(xt[:, u, :], x_words[:, 256 * kg + u : 256 * (kg + 1) : 2], ident_f[:])
+                dst = xg_words[:, 256 * kg : 256 * (kg + 1)].rearrange("p (k u) -> p k u", u=2)
+                src = xt[:].rearrange("p u k -> p k u")
+                if kg == 0:
+                    nc.vector.tensor_copy(out=dst, in_=src)
+                else:
+                    nc.scalar.copy(out=dst, in_=src)
+            nc.vector.quantize_mx(out=xq[i][:].bitcast(FP8X4), scales=xs[i][:], in_=xg[i][:])
+
+        hq = [keep.tile([P, M], U32, name="hq%d" % g, align_bytes=64) for g in range(KH)]
+        hs = [keep.tile([P, M], U8, name="hs%d" % g, align_bytes=64) for g in range(KH)]
+        h_tiles = {}
+        hg_tiles = {}
+
+        def unit(u):
+            g, i = divmod(u, TOK)
+            pair = u % 3
+            cols = slice(N * g, N * (g + 1))
+            acc_g = bank(2 * pair, [P, N], F32, "acc_g")
+            acc_u = bank(2 * pair + 1, [P, N], F32, "acc_u")
+            for acc, words, base in ((acc_g, gw, 0), (acc_u, uw, 8)):
+                for kg in range(KX):
+                    nc.tensor.matmul_mx(
+                        out=acc[:],
+                        lhsT=xq[i][:, P * kg : P * (kg + 1)].bitcast(FP8X4),
+                        lhsT_scale=xs[i][:, P * kg : P * (kg + 1)],
+                        rhs=words[g][:, kg, :].bitcast(FP8X4),
+                        rhs_scale=s1[base + 4 * kg : P, cols],
+                        start=(kg == 0),
+                        stop=(kg == KX - 1),
+                    )
+            sg = work.tile([P, 4, P], F32, name="sg", tag="sg", bufs=4)
+            nc.scalar.activation(out=sg[:], in_=acc_g[:].rearrange("p (m t) -> p t m", t=4), func=SILU)
+            h = work.tile([P, 4, P], BF16, name="h", tag="h", bufs=8)
+            nc.vector.tensor_tensor(out=h[:], in0=sg[:], in1=acc_u[:].rearrange("p (m t) -> p t m", t=4), op=MULT)
+            h_tiles[u] = h
+
+        def transposes(g):
+            hg = work.tile([P, M * 4], BF16, name="hg", tag="hg", bufs=2, align_bytes=64)
+            hg_tiles[g] = hg
+            for half in range(2):
+                ht = bank(6 + half, [P, 8, P], BF16, "ht")
+                for j in range(8):
+                    nc.tensor.transpose(ht[:, j, :], h_tiles[TOK * g + 2 * half + j // 4][:, j % 4, :], ident_b[:])
+                dst = hg[:, 1024 * half : 1024 * (half + 1)].rearrange("p (i k t) -> p i k t", i=2, t=4)
+                src = ht[:].rearrange("p (i t) k -> p i k t", t=4)
+                if half == 0:
+                    nc.scalar.copy(out=dst, in_=src)
+                else:
+                    nc.vector.tensor_copy(out=dst, in_=src)
+
+        def quantise(g):
+            nc.vector.quantize_mx(out=hq[g][:].bitcast(FP8X4), scales=hs[g][:], in_=hg_tiles[g][:])
+
+        for u in range(TOK * KH):
+            unit(u)
+            if u >= TOK and u % TOK == 1:
+                transposes(u // TOK - 1)
+            if u >= TOK and u % TOK == 2:
+                quantise(u // TOK - 1)
+
+        def down_pass(acc, i, dc, g):
+            nc.tensor.matmul_mx(
+                out=acc[:],
+                lhsT=hq[g][:, P * i : P * (i + 1)].bitcast(FP8X4),
+                lhsT_scale=hs[g][:, P * i : P * (i + 1)],
+                rhs=dw[g][:, N * dc : N * (dc + 1)].bitcast(FP8X4),
+                rhs_scale=s2[4 * (g % 4) : P, g // 4, N * dc : N * (dc + 1)],
+                start=(g == 0),
+                stop=(g == KH - 1),
+            )
+
+        def evacuate(acc, i, dc):
+            o = work.tile([P, N], F32, name="o", tag="o", bufs=8)
+            if dc == 0:
+                nc.vector.tensor_copy(out=o[:], in_=acc[:])
+            else:
+                nc.scalar.copy(out=o[:], in_=acc[:])
+            nc.sync.dma_start(out=out[P * i : P * (i + 1), N * dc : N * (dc + 1)], in_=o[:])
+
+        acc0 = [bank(2 + dc, [P, N], F32, "acc0") for dc in range(DC)]
+        for g in range(KH - 1):
+            for dc in range(DC):
+                down_pass(acc0[dc], 0, dc, g)
+        transposes(KH - 1)
+        quantise(KH - 1)
+        acc1 = [bank(4 + dc, [P, N], F32, "acc1") for dc in range(DC)]
+        for g in range(KH - 1):
+            for dc in range(DC):
+                down_pass(acc1[dc], 1, dc, g)
+        for i, accs in ((0, acc0), (1, acc1)):
+            for dc in range(DC):
+                down_pass(accs[dc], i, dc, KH - 1)
+                evacuate(accs[dc], i, dc)
+        for i, first in ((2, 0), (3, 6)):
+            for dc in range(DC):
+                acc = bank(first + dc, [P, N], F32, "acc")
+                for g in range(KH):
+                    down_pass(acc, i, dc, g)
+                evacuate(acc, i, dc)

@@ -20,6 +20,8 @@ KX = D // 512
 KH = F // 512
 DC = D // N
 
+S1_GROUPS = ((0, 1), (1, 3), (3, 7))
+
 FLOPS = 2 * M * D * F * 3
 
 
@@ -36,12 +38,14 @@ def tile_nvfp4persistentmlp_kernel(
         def bank(b, shape, dtype, name):
             return psum.tile(shape, dtype, name=name, tag="bank%d" % b)
 
-        s1 = keep.tile([P, F], U8, name="s1", align_bytes=64)
+        s1 = [keep.tile([P, N * (b - a)], U8, name="s1_%d" % a, align_bytes=64) for a, b in S1_GROUPS]
         s2 = keep.tile([P, 2, D], U8, name="s2", align_bytes=64)
         warm = keep.tile([P, 1], F32, name="warm")
         warm2 = keep.tile([P, 1], F32, name="warm2")
-        nc.vector.memset(s1[:].bitcast(I32), 0)
+        nc.vector.memset(s1[0][:].bitcast(I32), 0)
         nc.vector.memset(warm[:], 0.0)
+        nc.vector.memset(s1[1][:].bitcast(I32), 0)
+        nc.vector.memset(s1[2][:].bitcast(I32), 0)
         nc.vector.memset(s2[:].bitcast(I32), 0)
         nc.scalar.activation(out=warm2[:], in_=warm[:], func=SILU)
         ident_f = keep.tile([P, P], F32, name="ident_f")
@@ -55,7 +59,6 @@ def tile_nvfp4persistentmlp_kernel(
         dw = [keep.tile([P, D], U32, name="dw%d" % g, align_bytes=64) for g in range(KH)]
         gate_i32 = gate_words.rearrange("g p n t -> p g (n t)").bitcast(I32)
         up_i32 = up_words.rearrange("g p n t -> p g (n t)").bitcast(I32)
-        s1_i32 = s1[:].bitcast(I32)
         s2_i32 = s2[:].bitcast(I32)
         gs_i32 = gate_scales.bitcast(I32)
         us_i32 = up_scales.bitcast(I32)
@@ -64,17 +67,27 @@ def tile_nvfp4persistentmlp_kernel(
         def load_stage1_words(dst, src, g):
             nc.sync.dma_start(out=dst[g][:].bitcast(I32), in_=src[:, :, N * g : N * (g + 1)])
 
+        def load_stage1_scales(j, src, base):
+            a, b = S1_GROUPS[j]
+            dst = s1[j][:].bitcast(I32)
+            for q in range(4):
+                nc.sync.dma_start(
+                    out=dst[32 * q + base : 32 * q + base + 8, :],
+                    in_=src[:, 4 * q : 4 * q + 4, (N // 4) * a : (N // 4) * b],
+                )
+
         for i in range(TOK):
             nc.sync.dma_start(out=x_sb[i][:], in_=x[P * i : P * (i + 1), :])
+        load_stage1_scales(0, gs_i32, 0)
         load_stage1_words(gw, gate_i32, 0)
-        for q in range(4):
-            nc.sync.dma_start(out=s1_i32[32 * q : 32 * q + 8, :], in_=gs_i32[:, 4 * q : 4 * q + 4, :])
+        load_stage1_scales(0, us_i32, 8)
         load_stage1_words(uw, up_i32, 0)
-        for q in range(4):
-            nc.sync.dma_start(out=s1_i32[32 * q + 8 : 32 * q + 16, :], in_=us_i32[:, 4 * q : 4 * q + 4, :])
-        for g in range(1, KH):
-            load_stage1_words(gw, gate_i32, g)
-            load_stage1_words(uw, up_i32, g)
+        for j in range(1, len(S1_GROUPS)):
+            load_stage1_scales(j, gs_i32, 0)
+            load_stage1_scales(j, us_i32, 8)
+            for g in range(S1_GROUPS[j][0], S1_GROUPS[j][1]):
+                load_stage1_words(gw, gate_i32, g)
+                load_stage1_words(uw, up_i32, g)
         for g in range(KH):
             nc.sync.dma_start(
                 out=dw[g][:].bitcast(I32), in_=down_words[g].rearrange("p n t -> p (n t)").bitcast(I32)
@@ -110,7 +123,8 @@ def tile_nvfp4persistentmlp_kernel(
         def unit(u):
             g, i = divmod(u, TOK)
             pair = u % 3
-            cols = slice(N * g, N * (g + 1))
+            j = [a <= g < b for a, b in S1_GROUPS].index(True)
+            cols = slice(N * (g - S1_GROUPS[j][0]), N * (g - S1_GROUPS[j][0] + 1))
             acc_g = bank(2 * pair, [P, N], F32, "acc_g")
             acc_u = bank(2 * pair + 1, [P, N], F32, "acc_u")
             for acc, words, base in ((acc_g, gw, 0), (acc_u, uw, 8)):
@@ -120,7 +134,7 @@ def tile_nvfp4persistentmlp_kernel(
                         lhsT=xq[i][:, P * kg : P * (kg + 1)].bitcast(FP8X4),
                         lhsT_scale=xs[i][:, P * kg : P * (kg + 1)],
                         rhs=words[g][:, kg, :].bitcast(FP8X4),
-                        rhs_scale=s1[base + 4 * kg : P, cols],
+                        rhs_scale=s1[j][base + 4 * kg : P, cols],
                         start=(kg == 0),
                         stop=(kg == KX - 1),
                     )

@@ -19,7 +19,6 @@ TOK = M // P
 KX = D // 512
 KH = F // 512
 DC = D // N
-
 S1_GROUPS = ((0, 1), (1, 3), (3, 7))
 
 FLOPS = 2 * M * D * F * 3
@@ -38,10 +37,12 @@ def tile_nvfp4persistentmlp_kernel(
         def bank(b, shape, dtype, name):
             return psum.tile(shape, dtype, name=name, tag="bank%d" % b)
 
+        zeros = keep.tile([P, N], BF16, name="zeros")
         s1 = [keep.tile([P, N * (b - a)], U8, name="s1_%d" % a, align_bytes=64) for a, b in S1_GROUPS]
         s2 = keep.tile([P, 2, D], U8, name="s2", align_bytes=64)
         warm = keep.tile([P, 1], F32, name="warm")
         warm2 = keep.tile([P, 1], F32, name="warm2")
+        nc.vector.memset(zeros[:], 0.0)
         nc.vector.memset(s1[0][:].bitcast(I32), 0)
         nc.vector.memset(warm[:], 0.0)
         nc.vector.memset(s1[1][:].bitcast(I32), 0)
@@ -54,40 +55,48 @@ def tile_nvfp4persistentmlp_kernel(
         make_identity(nc, ident_b[:])
 
         x_sb = [keep.tile([P, D], BF16, name="x%d" % i) for i in range(TOK)]
-        gw = [keep.tile([P, KX, N], U32, name="gw%d" % g, align_bytes=64) for g in range(KH)]
-        uw = [keep.tile([P, KX, N], U32, name="uw%d" % g, align_bytes=64) for g in range(KH)]
-        dw = [keep.tile([P, D], U32, name="dw%d" % g, align_bytes=64) for g in range(KH)]
         gate_i32 = gate_words.rearrange("g p n t -> p g (n t)").bitcast(I32)
         up_i32 = up_words.rearrange("g p n t -> p g (n t)").bitcast(I32)
         s2_i32 = s2[:].bitcast(I32)
-        gs_i32 = gate_scales.bitcast(I32)
-        us_i32 = up_scales.bitcast(I32)
+        scales_i32 = (gate_scales.bitcast(I32), up_scales.bitcast(I32))
+        words_i32 = (gate_i32, up_i32)
         ds_i32 = down_scales.bitcast(I32)
+        words = {}
 
-        def load_stage1_words(dst, src, g):
-            nc.sync.dma_start(out=dst[g][:].bitcast(I32), in_=src[:, :, N * g : N * (g + 1)])
+        def load_stage1_words(which, g):
+            cols = slice(N * g, N * (g + 1))
+            if g == 0:
+                for kg in range(KX):
+                    t = keep.tile([P, N], U32, name="w%d_0_%d" % (which, kg), align_bytes=64)
+                    nc.sync.dma_start(out=t[:].bitcast(I32), in_=words_i32[which][:, kg, cols])
+                    words[(which, g, kg)] = t[:]
+            else:
+                t = keep.tile([P, KX, N], U32, name="w%d_%d" % (which, g), align_bytes=64)
+                nc.sync.dma_start(out=t[:].bitcast(I32), in_=words_i32[which][:, :, cols])
+                for kg in range(KX):
+                    words[(which, g, kg)] = t[:, kg, :]
 
-        def load_stage1_scales(j, src, base):
+        def load_stage1_scales(which, j):
             a, b = S1_GROUPS[j]
             dst = s1[j][:].bitcast(I32)
             for q in range(4):
                 nc.sync.dma_start(
-                    out=dst[32 * q + base : 32 * q + base + 8, :],
-                    in_=src[:, 4 * q : 4 * q + 4, (N // 4) * a : (N // 4) * b],
+                    out=dst[32 * q + 8 * which : 32 * q + 8 * which + 8, :],
+                    in_=scales_i32[which][:, 4 * q : 4 * q + 4, (N // 4) * a : (N // 4) * b],
                 )
 
         for i in range(TOK):
             nc.sync.dma_start(out=x_sb[i][:], in_=x[P * i : P * (i + 1), :])
-        load_stage1_scales(0, gs_i32, 0)
-        load_stage1_words(gw, gate_i32, 0)
-        load_stage1_scales(0, us_i32, 8)
-        load_stage1_words(uw, up_i32, 0)
+        for which in range(2):
+            load_stage1_scales(which, 0)
+            load_stage1_words(which, 0)
         for j in range(1, len(S1_GROUPS)):
-            load_stage1_scales(j, gs_i32, 0)
-            load_stage1_scales(j, us_i32, 8)
+            for which in range(2):
+                load_stage1_scales(which, j)
             for g in range(S1_GROUPS[j][0], S1_GROUPS[j][1]):
-                load_stage1_words(gw, gate_i32, g)
-                load_stage1_words(uw, up_i32, g)
+                for which in range(2):
+                    load_stage1_words(which, g)
+        dw = [keep.tile([P, D], U32, name="dw%d" % g, align_bytes=64) for g in range(KH)]
         for g in range(KH):
             nc.sync.dma_start(
                 out=dw[g][:].bitcast(I32), in_=down_words[g].rearrange("p n t -> p (n t)").bitcast(I32)
@@ -97,9 +106,16 @@ def tile_nvfp4persistentmlp_kernel(
         for q in range(4):
             nc.sync.dma_start(out=s2_i32[32 * q : 32 * q + 12, 1, :], in_=ds_i32[4:7, 4 * q : 4 * q + 4, :])
 
+        spare = bank(7, [P, N], F32, "spare")
+
+        def busy(n):
+            for rep in range(n):
+                nc.tensor.matmul(out=spare[:], lhsT=zeros[:, 0:P], rhs=zeros[:], start=True, stop=True)
+
         xq = [keep.tile([P, KX * P], U32, name="xq%d" % i, align_bytes=64) for i in range(TOK)]
         xs = [keep.tile([P, KX * P], U8, name="xs%d" % i, align_bytes=64) for i in range(TOK)]
         xg = [keep.tile([P, KX * P * 4], BF16, name="xg%d" % i, align_bytes=64) for i in range(TOK)]
+        busy(3)
         for i in range(TOK):
             x_words = x_sb[i][:].bitcast(F32)
             xg_words = xg[i][:].bitcast(F32)
@@ -114,34 +130,44 @@ def tile_nvfp4persistentmlp_kernel(
                 else:
                     nc.scalar.copy(out=dst, in_=src)
             nc.vector.quantize_mx(out=xq[i][:].bitcast(FP8X4), scales=xs[i][:], in_=xg[i][:])
+            if i < 2:
+                busy(1)
 
         hq = [keep.tile([P, M], U32, name="hq%d" % g, align_bytes=64) for g in range(KH)]
         hs = [keep.tile([P, M], U8, name="hs%d" % g, align_bytes=64) for g in range(KH)]
+        accs = {}
+        sg_tiles = {}
         h_tiles = {}
         hg_tiles = {}
 
-        def unit(u):
+        def open_unit(u):
+            pair = u if u < TOK else (u - TOK) % 3
+            accs[u] = (bank(2 * pair, [P, N], F32, "acc_g"), bank(2 * pair + 1, [P, N], F32, "acc_u"))
+
+        def stage1_pass(u, which, kg):
             g, i = divmod(u, TOK)
-            pair = u % 3
             j = [a <= g < b for a, b in S1_GROUPS].index(True)
-            cols = slice(N * (g - S1_GROUPS[j][0]), N * (g - S1_GROUPS[j][0] + 1))
-            acc_g = bank(2 * pair, [P, N], F32, "acc_g")
-            acc_u = bank(2 * pair + 1, [P, N], F32, "acc_u")
-            for acc, words, base in ((acc_g, gw, 0), (acc_u, uw, 8)):
-                for kg in range(KX):
-                    nc.tensor.matmul_mx(
-                        out=acc[:],
-                        lhsT=xq[i][:, P * kg : P * (kg + 1)].bitcast(FP8X4),
-                        lhsT_scale=xs[i][:, P * kg : P * (kg + 1)],
-                        rhs=words[g][:, kg, :].bitcast(FP8X4),
-                        rhs_scale=s1[j][base + 4 * kg : P, cols],
-                        start=(kg == 0),
-                        stop=(kg == KX - 1),
-                    )
+            first = N * (g - S1_GROUPS[j][0])
+            nc.tensor.matmul_mx(
+                out=accs[u][which][:],
+                lhsT=xq[i][:, P * kg : P * (kg + 1)].bitcast(FP8X4),
+                lhsT_scale=xs[i][:, P * kg : P * (kg + 1)],
+                rhs=words[(which, g, kg)].bitcast(FP8X4),
+                rhs_scale=s1[j][8 * which + 4 * kg : P, first : first + N],
+                start=(kg == 0),
+                stop=(kg == KX - 1),
+            )
+
+        def silu(u):
             sg = work.tile([P, 4, P], F32, name="sg", tag="sg", bufs=4)
-            nc.scalar.activation(out=sg[:], in_=acc_g[:].rearrange("p (m t) -> p t m", t=4), func=SILU)
+            nc.scalar.activation(out=sg[:], in_=accs[u][0][:].rearrange("p (m t) -> p t m", t=4), func=SILU)
+            sg_tiles[u] = sg
+
+        def gate(u):
             h = work.tile([P, 4, P], BF16, name="h", tag="h", bufs=8)
-            nc.vector.tensor_tensor(out=h[:], in0=sg[:], in1=acc_u[:].rearrange("p (m t) -> p t m", t=4), op=MULT)
+            nc.vector.tensor_tensor(
+                out=h[:], in0=sg_tiles[u][:], in1=accs[u][1][:].rearrange("p (m t) -> p t m", t=4), op=MULT
+            )
             h_tiles[u] = h
 
         def transposes(g):
@@ -161,11 +187,27 @@ def tile_nvfp4persistentmlp_kernel(
         def quantise(g):
             nc.vector.quantize_mx(out=hq[g][:].bitcast(FP8X4), scales=hs[g][:], in_=hg_tiles[g][:])
 
-        for u in range(TOK * KH):
-            unit(u)
-            if u >= TOK and u % TOK == 1:
+        for u in range(TOK):
+            open_unit(u)
+        for which in range(2):
+            for kg in range(KX):
+                for u in range(TOK):
+                    stage1_pass(u, which, kg)
+            for u in range(TOK):
+                if which == 0:
+                    silu(u)
+                else:
+                    gate(u)
+        for u in range(TOK, TOK * KH):
+            open_unit(u)
+            for which in range(2):
+                for kg in range(KX):
+                    stage1_pass(u, which, kg)
+            silu(u)
+            gate(u)
+            if u % TOK == 1:
                 transposes(u // TOK - 1)
-            if u >= TOK and u % TOK == 2:
+            if u % TOK == 2:
                 quantise(u // TOK - 1)
 
         def down_pass(acc, i, dc, g):
@@ -187,23 +229,23 @@ def tile_nvfp4persistentmlp_kernel(
                 nc.scalar.copy(out=o[:], in_=acc[:])
             nc.sync.dma_start(out=out[P * i : P * (i + 1), N * dc : N * (dc + 1)], in_=o[:])
 
-        acc0 = [bank(2 + dc, [P, N], F32, "acc0") for dc in range(DC)]
+        acc0 = [bank(0 + dc, [P, N], F32, "acc0") for dc in range(DC)]
         for g in range(KH - 1):
             for dc in range(DC):
                 down_pass(acc0[dc], 0, dc, g)
         transposes(KH - 1)
         quantise(KH - 1)
-        acc1 = [bank(4 + dc, [P, N], F32, "acc1") for dc in range(DC)]
+        acc1 = [bank(2 + dc, [P, N], F32, "acc1") for dc in range(DC)]
         for g in range(KH - 1):
             for dc in range(DC):
                 down_pass(acc1[dc], 1, dc, g)
-        for i, accs in ((0, acc0), (1, acc1)):
+        for i, pair_accs in ((0, acc0), (1, acc1)):
             for dc in range(DC):
-                down_pass(accs[dc], i, dc, KH - 1)
-                evacuate(accs[dc], i, dc)
-        for i, first in ((2, 0), (3, 6)):
+                down_pass(pair_accs[dc], i, dc, KH - 1)
+                evacuate(pair_accs[dc], i, dc)
+        for i, first_bank in ((2, 4), (3, 6)):
             for dc in range(DC):
-                acc = bank(first + dc, [P, N], F32, "acc")
+                acc = bank(first_bank + dc, [P, N], F32, "acc")
                 for g in range(KH):
                     down_pass(acc, i, dc, g)
                 evacuate(acc, i, dc)

@@ -19,7 +19,7 @@ TOK = M // P
 KX = D // 512
 KH = F // 512
 DC = D // N
-S1_GROUPS = ((0, 1), (1, 3), (3, 7))
+S1_GROUPS = ((0, 2), (2, 7))
 
 FLOPS = 2 * M * D * F * 3
 
@@ -46,7 +46,6 @@ def tile_nvfp4persistentmlp_kernel(
         nc.vector.memset(s1[0][:].bitcast(I32), 0)
         nc.vector.memset(warm[:], 0.0)
         nc.vector.memset(s1[1][:].bitcast(I32), 0)
-        nc.vector.memset(s1[2][:].bitcast(I32), 0)
         nc.vector.memset(s2[:].bitcast(I32), 0)
         nc.scalar.activation(out=warm2[:], in_=warm[:], func=SILU)
         ident_f = keep.tile([P, P], F32, name="ident_f")
@@ -57,10 +56,10 @@ def tile_nvfp4persistentmlp_kernel(
         x_sb = [keep.tile([P, D], BF16, name="x%d" % i) for i in range(TOK)]
         gate_i32 = gate_words.rearrange("g p n t -> p g (n t)").bitcast(I32)
         up_i32 = up_words.rearrange("g p n t -> p g (n t)").bitcast(I32)
-        s2_i32 = s2[:].bitcast(I32)
-        scales_i32 = (gate_scales.bitcast(I32), up_scales.bitcast(I32))
+        s2_f32 = s2[:].bitcast(F32)
+        scales_dram = (gate_scales, up_scales)
         words_i32 = (gate_i32, up_i32)
-        ds_i32 = down_scales.bitcast(I32)
+        ds_f32 = down_scales.bitcast(F32)
         words = {}
 
         def load_stage1_words(which, g):
@@ -78,11 +77,13 @@ def tile_nvfp4persistentmlp_kernel(
 
         def load_stage1_scales(which, j):
             a, b = S1_GROUPS[j]
-            dst = s1[j][:].bitcast(I32)
+            queue, view = ((nc.sync, I32), (nc.gpsimd, F32))[j]
+            dst = s1[j][:].bitcast(view)
+            src = scales_dram[which].bitcast(view)
             for q in range(4):
-                nc.sync.dma_start(
+                queue.dma_start(
                     out=dst[32 * q + 8 * which : 32 * q + 8 * which + 8, :],
-                    in_=scales_i32[which][:, 4 * q : 4 * q + 4, (N // 4) * a : (N // 4) * b],
+                    in_=src[:, 4 * q : 4 * q + 4, (N // 4) * a : (N // 4) * b],
                 )
 
         for i in range(TOK):
@@ -90,21 +91,20 @@ def tile_nvfp4persistentmlp_kernel(
         for which in range(2):
             load_stage1_scales(which, 0)
             load_stage1_words(which, 0)
-        for j in range(1, len(S1_GROUPS)):
+        for which in range(2):
+            load_stage1_scales(which, 1)
+        for g in range(1, KH):
             for which in range(2):
-                load_stage1_scales(which, j)
-            for g in range(S1_GROUPS[j][0], S1_GROUPS[j][1]):
-                for which in range(2):
-                    load_stage1_words(which, g)
+                load_stage1_words(which, g)
         dw = [keep.tile([P, D], U32, name="dw%d" % g, align_bytes=64) for g in range(KH)]
         for g in range(KH):
             nc.sync.dma_start(
                 out=dw[g][:].bitcast(I32), in_=down_words[g].rearrange("p n t -> p (n t)").bitcast(I32)
             )
         for q in range(4):
-            nc.sync.dma_start(out=s2_i32[32 * q : 32 * q + 16, 0, :], in_=ds_i32[0:4, 4 * q : 4 * q + 4, :])
+            nc.gpsimd.dma_start(out=s2_f32[32 * q : 32 * q + 16, 0, :], in_=ds_f32[0:4, 4 * q : 4 * q + 4, :])
         for q in range(4):
-            nc.sync.dma_start(out=s2_i32[32 * q : 32 * q + 12, 1, :], in_=ds_i32[4:7, 4 * q : 4 * q + 4, :])
+            nc.gpsimd.dma_start(out=s2_f32[32 * q : 32 * q + 12, 1, :], in_=ds_f32[4:7, 4 * q : 4 * q + 4, :])
 
         spare = bank(7, [P, N], F32, "spare")
 
@@ -210,42 +210,48 @@ def tile_nvfp4persistentmlp_kernel(
             if u % TOK == 2:
                 quantise(u // TOK - 1)
 
-        def down_pass(acc, i, dc, g):
+        def down_pass(acc, i, c0, width, g):
             nc.tensor.matmul_mx(
                 out=acc[:],
                 lhsT=hq[g][:, P * i : P * (i + 1)].bitcast(FP8X4),
                 lhsT_scale=hs[g][:, P * i : P * (i + 1)],
-                rhs=dw[g][:, N * dc : N * (dc + 1)].bitcast(FP8X4),
-                rhs_scale=s2[4 * (g % 4) : P, g // 4, N * dc : N * (dc + 1)],
+                rhs=dw[g][:, c0 : c0 + width].bitcast(FP8X4),
+                rhs_scale=s2[4 * (g % 4) : P, g // 4, c0 : c0 + width],
                 start=(g == 0),
                 stop=(g == KH - 1),
             )
 
-        def evacuate(acc, i, dc):
-            o = work.tile([P, N], F32, name="o", tag="o", bufs=8)
-            if dc == 0:
+        def evacuate(acc, i, c0, width, on_vector):
+            o = work.tile([P, width], F32, name="o", tag="o", bufs=9)
+            if on_vector:
                 nc.vector.tensor_copy(out=o[:], in_=acc[:])
             else:
                 nc.scalar.copy(out=o[:], in_=acc[:])
-            nc.sync.dma_start(out=out[P * i : P * (i + 1), N * dc : N * (dc + 1)], in_=o[:])
+            nc.sync.dma_start(out=out[P * i : P * (i + 1), c0 : c0 + width], in_=o[:])
 
         acc0 = [bank(0 + dc, [P, N], F32, "acc0") for dc in range(DC)]
         for g in range(KH - 1):
             for dc in range(DC):
-                down_pass(acc0[dc], 0, dc, g)
+                down_pass(acc0[dc], 0, N * dc, N, g)
         transposes(KH - 1)
         quantise(KH - 1)
         acc1 = [bank(2 + dc, [P, N], F32, "acc1") for dc in range(DC)]
         for g in range(KH - 1):
             for dc in range(DC):
-                down_pass(acc1[dc], 1, dc, g)
+                down_pass(acc1[dc], 1, N * dc, N, g)
         for i, pair_accs in ((0, acc0), (1, acc1)):
             for dc in range(DC):
-                down_pass(pair_accs[dc], i, dc, KH - 1)
-                evacuate(pair_accs[dc], i, dc)
-        for i, first_bank in ((2, 4), (3, 6)):
-            for dc in range(DC):
-                acc = bank(first_bank + dc, [P, N], F32, "acc")
-                for g in range(KH):
-                    down_pass(acc, i, dc, g)
-                evacuate(acc, i, dc)
+                down_pass(pair_accs[dc], i, N * dc, N, KH - 1)
+                evacuate(pair_accs[dc], i, N * dc, N, dc == 0)
+        last = (
+            (2, 4, 0, N, True),
+            (2, 5, N, N, False),
+            (3, 6, 0, N, True),
+            (3, 7, N, N // 2, False),
+            (3, 0, N + N // 2, N // 2, True),
+        )
+        for i, b, c0, width, on_vector in last:
+            acc = bank(b, [P, width], F32, "acc")
+            for g in range(KH):
+                down_pass(acc, i, c0, width, g)
+            evacuate(acc, i, c0, width, on_vector)

@@ -19,7 +19,7 @@ TOK = M // P
 KX = D // 512
 KH = F // 512
 DC = D // N
-S1_GROUPS = ((0, 2), (2, 7))
+S1_GROUPS = ((0, 1), (1, 2), (2, 3), (3, 5), (5, 7))
 
 FLOPS = 2 * M * D * F * 3
 
@@ -45,7 +45,8 @@ def tile_nvfp4persistentmlp_kernel(
         nc.vector.memset(zeros[:], 0.0)
         nc.vector.memset(s1[0][:].bitcast(I32), 0)
         nc.vector.memset(warm[:], 0.0)
-        nc.vector.memset(s1[1][:].bitcast(I32), 0)
+        for j in range(1, len(S1_GROUPS)):
+            nc.vector.memset(s1[j][:].bitcast(I32), 0)
         nc.vector.memset(s2[:].bitcast(I32), 0)
         nc.scalar.activation(out=warm2[:], in_=warm[:], func=SILU)
         ident_f = keep.tile([P, P], F32, name="ident_f")
@@ -56,10 +57,10 @@ def tile_nvfp4persistentmlp_kernel(
         x_sb = [keep.tile([P, D], BF16, name="x%d" % i) for i in range(TOK)]
         gate_i32 = gate_words.rearrange("g p n t -> p g (n t)").bitcast(I32)
         up_i32 = up_words.rearrange("g p n t -> p g (n t)").bitcast(I32)
-        s2_f32 = s2[:].bitcast(F32)
-        scales_dram = (gate_scales, up_scales)
+        s2_i32 = s2[:].bitcast(I32)
+        scales_i32 = (gate_scales.bitcast(I32), up_scales.bitcast(I32))
         words_i32 = (gate_i32, up_i32)
-        ds_f32 = down_scales.bitcast(F32)
+        ds_i32 = down_scales.bitcast(I32)
         words = {}
 
         def load_stage1_words(which, g):
@@ -77,34 +78,31 @@ def tile_nvfp4persistentmlp_kernel(
 
         def load_stage1_scales(which, j):
             a, b = S1_GROUPS[j]
-            queue, view = ((nc.sync, I32), (nc.gpsimd, F32))[j]
-            dst = s1[j][:].bitcast(view)
-            src = scales_dram[which].bitcast(view)
+            dst = s1[j][:].bitcast(I32)
             for q in range(4):
-                queue.dma_start(
+                nc.sync.dma_start(
                     out=dst[32 * q + 8 * which : 32 * q + 8 * which + 8, :],
-                    in_=src[:, 4 * q : 4 * q + 4, (N // 4) * a : (N // 4) * b],
+                    in_=scales_i32[which][:, 4 * q : 4 * q + 4, (N // 4) * a : (N // 4) * b],
                 )
 
         for i in range(TOK):
             nc.sync.dma_start(out=x_sb[i][:], in_=x[P * i : P * (i + 1), :])
-        for which in range(2):
-            load_stage1_scales(which, 0)
-            load_stage1_words(which, 0)
-        for which in range(2):
-            load_stage1_scales(which, 1)
-        for g in range(1, KH):
+        for j, (a, b) in enumerate(S1_GROUPS):
             for which in range(2):
-                load_stage1_words(which, g)
+                load_stage1_scales(which, j)
+                load_stage1_words(which, a)
+            for g in range(a + 1, b):
+                for which in range(2):
+                    load_stage1_words(which, g)
         dw = [keep.tile([P, D], U32, name="dw%d" % g, align_bytes=64) for g in range(KH)]
         for g in range(KH):
             nc.sync.dma_start(
                 out=dw[g][:].bitcast(I32), in_=down_words[g].rearrange("p n t -> p (n t)").bitcast(I32)
             )
         for q in range(4):
-            nc.gpsimd.dma_start(out=s2_f32[32 * q : 32 * q + 16, 0, :], in_=ds_f32[0:4, 4 * q : 4 * q + 4, :])
+            nc.sync.dma_start(out=s2_i32[32 * q : 32 * q + 16, 0, :], in_=ds_i32[0:4, 4 * q : 4 * q + 4, :])
         for q in range(4):
-            nc.gpsimd.dma_start(out=s2_f32[32 * q : 32 * q + 12, 1, :], in_=ds_f32[4:7, 4 * q : 4 * q + 4, :])
+            nc.sync.dma_start(out=s2_i32[32 * q : 32 * q + 12, 1, :], in_=ds_i32[4:7, 4 * q : 4 * q + 4, :])
 
         spare = bank(7, [P, N], F32, "spare")
 
@@ -198,13 +196,27 @@ def tile_nvfp4persistentmlp_kernel(
                     silu(u)
                 else:
                     gate(u)
-        for u in range(TOK, TOK * KH):
+        early = range(TOK, TOK + 3)
+        for u in early:
+            open_unit(u)
+        for which in range(2):
+            for u in early:
+                for kg in range(KX):
+                    stage1_pass(u, which, kg)
+                if which == 0:
+                    silu(u)
+                else:
+                    gate(u)
+        transposes(0)
+        for u in range(TOK + 3, TOK * KH):
             open_unit(u)
             for which in range(2):
                 for kg in range(KX):
                     stage1_pass(u, which, kg)
             silu(u)
             gate(u)
+            if u == TOK + 3:
+                quantise(0)
             if u % TOK == 1:
                 transposes(u // TOK - 1)
             if u % TOK == 2:

@@ -88,6 +88,11 @@ def tile_nvfp4persistentmlp_kernel(
         for i in range(TOK):
             nc.sync.dma_start(out=x_sb[i][:], in_=x[P * i : P * (i + 1), :])
         for j, (a, b) in enumerate(S1_GROUPS):
+            if j == len(S1_GROUPS) - 1:
+                for q in range(4):
+                    nc.sync.dma_start(out=s2_i32[32 * q : 32 * q + 16, 0, :], in_=ds_i32[0:4, 4 * q : 4 * q + 4, :])
+                for q in range(4):
+                    nc.sync.dma_start(out=s2_i32[32 * q : 32 * q + 12, 1, :], in_=ds_i32[4:7, 4 * q : 4 * q + 4, :])
             for which in range(2):
                 load_stage1_scales(which, j)
                 load_stage1_words(which, a)
@@ -99,10 +104,6 @@ def tile_nvfp4persistentmlp_kernel(
             nc.sync.dma_start(
                 out=dw[g][:].bitcast(I32), in_=down_words[g].rearrange("p n t -> p (n t)").bitcast(I32)
             )
-        for q in range(4):
-            nc.sync.dma_start(out=s2_i32[32 * q : 32 * q + 16, 0, :], in_=ds_i32[0:4, 4 * q : 4 * q + 4, :])
-        for q in range(4):
-            nc.sync.dma_start(out=s2_i32[32 * q : 32 * q + 12, 1, :], in_=ds_i32[4:7, 4 * q : 4 * q + 4, :])
 
         spare = bank(7, [P, N], F32, "spare")
 
@@ -242,15 +243,14 @@ def tile_nvfp4persistentmlp_kernel(
             nc.sync.dma_start(out=out[P * i : P * (i + 1), c0 : c0 + width], in_=o[:])
 
         acc0 = [bank(0 + dc, [P, N], F32, "acc0") for dc in range(DC)]
-        for g in range(KH - 1):
-            for dc in range(DC):
-                down_pass(acc0[dc], 0, N * dc, N, g)
-        transposes(KH - 1)
-        quantise(KH - 1)
         acc1 = [bank(2 + dc, [P, N], F32, "acc1") for dc in range(DC)]
         for g in range(KH - 1):
-            for dc in range(DC):
-                down_pass(acc1[dc], 1, N * dc, N, g)
+            if g == (KH - 1) // 2:
+                transposes(KH - 1)
+                quantise(KH - 1)
+            for i, pair_accs in ((0, acc0), (1, acc1)):
+                for dc in range(DC):
+                    down_pass(pair_accs[dc], i, N * dc, N, g)
         for i, pair_accs in ((0, acc0), (1, acc1)):
             for dc in range(DC):
                 down_pass(pair_accs[dc], i, N * dc, N, KH - 1)

@@ -1,7 +1,6 @@
 from contextlib import ExitStack
 
 import concourse.mybir as mybir
-from concourse.masks import make_identity
 
 F32 = mybir.dt.float32
 BF16 = mybir.dt.bfloat16
@@ -11,6 +10,8 @@ U8 = mybir.dt.uint8
 FP8X4 = mybir.dt.float8_e4m3fn_x4
 SILU = mybir.ActivationFunctionType.Silu
 MULT = mybir.AluOpType.mult
+ADD = mybir.AluOpType.add
+IS_EQUAL = mybir.AluOpType.is_equal
 
 P = 128
 M, D, F = 512, 1024, 3584
@@ -37,22 +38,29 @@ def tile_nvfp4persistentmlp_kernel(
         def bank(b, shape, dtype, name):
             return psum.tile(shape, dtype, name=name, tag="bank%d" % b)
 
-        zeros = keep.tile([P, N], BF16, name="zeros")
+        ones = keep.tile([P, P], BF16, name="ones")
+        share = keep.tile([P, N], BF16, name="share")
+        ramp = keep.tile([P, P], BF16, name="ramp")
         s1 = [keep.tile([P, N * (b - a)], U8, name="s1_%d" % a, align_bytes=64) for a, b in S1_GROUPS]
         s2 = keep.tile([P, 2, D], U8, name="s2", align_bytes=64)
         warm = keep.tile([P, 1], F32, name="warm")
         warm2 = keep.tile([P, 1], F32, name="warm2")
-        nc.vector.memset(zeros[:], 0.0)
-        nc.vector.memset(s1[0][:].bitcast(I32), 0)
+        ident_f = keep.tile([P, P], F32, name="ident_f")
+        ident_b = keep.tile([P, P], BF16, name="ident_b")
         nc.vector.memset(warm[:], 0.0)
-        for j in range(1, len(S1_GROUPS)):
+        nc.vector.memset(ones[:], 1.0)
+        nc.vector.memset(share[:], 1.0 / P)
+        nc.vector.tensor_tensor_scan(out=ramp[:], data0=ones[:], data1=ones[:], initial=0.0, op0=MULT, op1=ADD)
+        row_index = bank(6, [P, N], F32, "row_index")
+        nc.tensor.matmul(out=row_index[:], lhsT=ramp[:], rhs=share[:], start=True, stop=True)
+        nc.vector.memset(s1[0][:].bitcast(I32), 0)
+        nc.vector.memset(s1[1][:].bitcast(I32), 0)
+        nc.vector.tensor_tensor(out=ident_f[:], in0=row_index[:, 0:P], in1=ramp[:], op=IS_EQUAL)
+        nc.vector.tensor_tensor(out=ident_b[:], in0=row_index[:, 0:P], in1=ramp[:], op=IS_EQUAL)
+        for j in range(2, len(S1_GROUPS)):
             nc.vector.memset(s1[j][:].bitcast(I32), 0)
         nc.vector.memset(s2[:].bitcast(I32), 0)
         nc.scalar.activation(out=warm2[:], in_=warm[:], func=SILU)
-        ident_f = keep.tile([P, P], F32, name="ident_f")
-        ident_b = keep.tile([P, P], BF16, name="ident_b")
-        make_identity(nc, ident_f[:])
-        make_identity(nc, ident_b[:])
 
         x_sb = [keep.tile([P, D], BF16, name="x%d" % i) for i in range(TOK)]
         gate_i32 = gate_words.rearrange("g p n t -> p g (n t)").bitcast(I32)
@@ -109,12 +117,12 @@ def tile_nvfp4persistentmlp_kernel(
 
         def busy(n):
             for rep in range(n):
-                nc.tensor.matmul(out=spare[:], lhsT=zeros[:, 0:P], rhs=zeros[:], start=True, stop=True)
+                nc.tensor.matmul(out=spare[:], lhsT=ramp[:], rhs=share[:], start=True, stop=True)
 
         xq = [keep.tile([P, KX * P], U32, name="xq%d" % i, align_bytes=64) for i in range(TOK)]
         xs = [keep.tile([P, KX * P], U8, name="xs%d" % i, align_bytes=64) for i in range(TOK)]
         xg = [keep.tile([P, KX * P * 4], BF16, name="xg%d" % i, align_bytes=64) for i in range(TOK)]
-        busy(3)
+        busy(2)
         for i in range(TOK):
             x_words = x_sb[i][:].bitcast(F32)
             xg_words = xg[i][:].bitcast(F32)

from contextlib import ExitStack

import concourse.mybir as mybir

F32 = mybir.dt.float32
BF16 = mybir.dt.bfloat16
I32 = mybir.dt.int32
U32 = mybir.dt.uint32
U8 = mybir.dt.uint8
FP8X4 = mybir.dt.float8_e4m3fn_x4
SILU = mybir.ActivationFunctionType.Silu
MULT = mybir.AluOpType.mult
ADD = mybir.AluOpType.add
IS_EQUAL = mybir.AluOpType.is_equal

P = 128
M, D, F = 512, 1024, 3584
N = 512
TOK = M // P
KX = D // 512
KH = F // 512
DC = D // N
S1_GROUPS = ((0, 1), (1, 2), (2, 3), (3, 5), (5, 7))

FLOPS = 2 * M * D * F * 3


def tile_nvfp4persistentmlp_kernel(
    tc, x, gate_words, gate_scales, up_words, up_scales, down_words, down_scales, out
):
    nc = tc.nc
    with ExitStack() as ctx:
        keep = ctx.enter_context(tc.tile_pool(name="keep", bufs=1))
        work = ctx.enter_context(tc.tile_pool(name="work", bufs=1))
        psum = ctx.enter_context(tc.psum_pool(name="psum", bufs=1))
        ctx.enter_context(tc.manual_schedule())

        def bank(b, shape, dtype, name):
            return psum.tile(shape, dtype, name=name, tag="bank%d" % b)

        ones = keep.tile([P, P], BF16, name="ones")
        share = keep.tile([P, N], BF16, name="share")
        ramp = keep.tile([P, P], BF16, name="ramp")
        s1 = [keep.tile([P, N * (b - a)], U8, name="s1_%d" % a, align_bytes=64) for a, b in S1_GROUPS]
        s2 = keep.tile([P, 2, D], U8, name="s2", align_bytes=64)
        warm = keep.tile([P, 1], F32, name="warm")
        warm2 = keep.tile([P, 1], F32, name="warm2")
        ident_f = keep.tile([P, P], F32, name="ident_f")
        ident_b = keep.tile([P, P], BF16, name="ident_b")
        nc.vector.memset(warm[:], 0.0)
        nc.vector.memset(ones[:], 1.0)
        nc.vector.memset(share[:], 1.0 / P)
        nc.vector.tensor_tensor_scan(out=ramp[:], data0=ones[:], data1=ones[:], initial=0.0, op0=MULT, op1=ADD)
        row_index = bank(6, [P, N], F32, "row_index")
        nc.tensor.matmul(out=row_index[:], lhsT=ramp[:], rhs=share[:], start=True, stop=True)
        nc.vector.memset(s1[0][:].bitcast(I32), 0)
        nc.vector.memset(s1[1][:].bitcast(I32), 0)
        nc.vector.tensor_tensor(out=ident_f[:], in0=row_index[:, 0:P], in1=ramp[:], op=IS_EQUAL)
        nc.vector.tensor_tensor(out=ident_b[:], in0=row_index[:, 0:P], in1=ramp[:], op=IS_EQUAL)
        for j in range(2, len(S1_GROUPS)):
            nc.vector.memset(s1[j][:].bitcast(I32), 0)
        nc.vector.memset(s2[:].bitcast(I32), 0)
        nc.scalar.activation(out=warm2[:], in_=warm[:], func=SILU)

        x_sb = [keep.tile([P, D], BF16, name="x%d" % i) for i in range(TOK)]
        gate_i32 = gate_words.rearrange("g p n t -> p g (n t)").bitcast(I32)
        up_i32 = up_words.rearrange("g p n t -> p g (n t)").bitcast(I32)
        s2_i32 = s2[:].bitcast(I32)
        scales_i32 = (gate_scales.bitcast(I32), up_scales.bitcast(I32))
        words_i32 = (gate_i32, up_i32)
        ds_i32 = down_scales.bitcast(I32)
        words = {}

        def load_stage1_words(which, g):
            cols = slice(N * g, N * (g + 1))
            if g == 0:
                for kg in range(KX):
                    t = keep.tile([P, N], U32, name="w%d_0_%d" % (which, kg), align_bytes=64)
                    nc.sync.dma_start(out=t[:].bitcast(I32), in_=words_i32[which][:, kg, cols])
                    words[(which, g, kg)] = t[:]
            else:
                t = keep.tile([P, KX, N], U32, name="w%d_%d" % (which, g), align_bytes=64)
                nc.sync.dma_start(out=t[:].bitcast(I32), in_=words_i32[which][:, :, cols])
                for kg in range(KX):
                    words[(which, g, kg)] = t[:, kg, :]

        def load_stage1_scales(which, j):
            a, b = S1_GROUPS[j]
            dst = s1[j][:].bitcast(I32)
            for q in range(4):
                nc.sync.dma_start(
                    out=dst[32 * q + 8 * which : 32 * q + 8 * which + 8, :],
                    in_=scales_i32[which][:, 4 * q : 4 * q + 4, (N // 4) * a : (N // 4) * b],
                )

        for i in range(TOK):
            nc.sync.dma_start(out=x_sb[i][:], in_=x[P * i : P * (i + 1), :])
        for j, (a, b) in enumerate(S1_GROUPS):
            if j == len(S1_GROUPS) - 1:
                for q in range(4):
                    nc.sync.dma_start(out=s2_i32[32 * q : 32 * q + 16, 0, :], in_=ds_i32[0:4, 4 * q : 4 * q + 4, :])
                for q in range(4):
                    nc.sync.dma_start(out=s2_i32[32 * q : 32 * q + 12, 1, :], in_=ds_i32[4:7, 4 * q : 4 * q + 4, :])
            for which in range(2):
                load_stage1_scales(which, j)
                load_stage1_words(which, a)
            for g in range(a + 1, b):
                for which in range(2):
                    load_stage1_words(which, g)
        dw = [keep.tile([P, D], U32, name="dw%d" % g, align_bytes=64) for g in range(KH)]
        for g in range(KH):
            nc.sync.dma_start(
                out=dw[g][:].bitcast(I32), in_=down_words[g].rearrange("p n t -> p (n t)").bitcast(I32)
            )

        spare = bank(7, [P, N], F32, "spare")

        def busy(n):
            for rep in range(n):
                nc.tensor.matmul(out=spare[:], lhsT=ramp[:], rhs=share[:], start=True, stop=True)

        xq = [keep.tile([P, KX * P], U32, name="xq%d" % i, align_bytes=64) for i in range(TOK)]
        xs = [keep.tile([P, KX * P], U8, name="xs%d" % i, align_bytes=64) for i in range(TOK)]
        xg = [keep.tile([P, KX * P * 4], BF16, name="xg%d" % i, align_bytes=64) for i in range(TOK)]
        busy(2)
        for i in range(TOK):
            x_words = x_sb[i][:].bitcast(F32)
            xg_words = xg[i][:].bitcast(F32)
            for kg in range(KX):
                xt = bank(2 * i + kg, [P, 2, P], F32, "xt")
                for u in range(2):
                    nc.tensor.transpose(xt[:, u, :], x_words[:, 256 * kg + u : 256 * (kg + 1) : 2], ident_f[:])
                dst = xg_words[:, 256 * kg : 256 * (kg + 1)].rearrange("p (k u) -> p k u", u=2)
                src = xt[:].rearrange("p u k -> p k u")
                if kg == 0:
                    nc.vector.tensor_copy(out=dst, in_=src)
                else:
                    nc.scalar.copy(out=dst, in_=src)
            nc.vector.quantize_mx(out=xq[i][:].bitcast(FP8X4), scales=xs[i][:], in_=xg[i][:])
            if i < 2:
                busy(1)

        hq = [keep.tile([P, M], U32, name="hq%d" % g, align_bytes=64) for g in range(KH)]
        hs = [keep.tile([P, M], U8, name="hs%d" % g, align_bytes=64) for g in range(KH)]
        accs = {}
        sg_tiles = {}
        h_tiles = {}
        hg_tiles = {}

        def open_unit(u):
            pair = u if u < TOK else (u - TOK) % 3
            accs[u] = (bank(2 * pair, [P, N], F32, "acc_g"), bank(2 * pair + 1, [P, N], F32, "acc_u"))

        def stage1_pass(u, which, kg):
            g, i = divmod(u, TOK)
            j = [a <= g < b for a, b in S1_GROUPS].index(True)
            first = N * (g - S1_GROUPS[j][0])
            nc.tensor.matmul_mx(
                out=accs[u][which][:],
                lhsT=xq[i][:, P * kg : P * (kg + 1)].bitcast(FP8X4),
                lhsT_scale=xs[i][:, P * kg : P * (kg + 1)],
                rhs=words[(which, g, kg)].bitcast(FP8X4),
                rhs_scale=s1[j][8 * which + 4 * kg : P, first : first + N],
                start=(kg == 0),
                stop=(kg == KX - 1),
            )

        def silu(u):
            sg = work.tile([P, 4, P], F32, name="sg", tag="sg", bufs=4)
            nc.scalar.activation(out=sg[:], in_=accs[u][0][:].rearrange("p (m t) -> p t m", t=4), func=SILU)
            sg_tiles[u] = sg

        def gate(u):
            h = work.tile([P, 4, P], BF16, name="h", tag="h", bufs=8)
            nc.vector.tensor_tensor(
                out=h[:], in0=sg_tiles[u][:], in1=accs[u][1][:].rearrange("p (m t) -> p t m", t=4), op=MULT
            )
            h_tiles[u] = h

        def transposes(g):
            hg = work.tile([P, M * 4], BF16, name="hg", tag="hg", bufs=2, align_bytes=64)
            hg_tiles[g] = hg
            for half in range(2):
                ht = bank(6 + half, [P, 8, P], BF16, "ht")
                for j in range(8):
                    nc.tensor.transpose(ht[:, j, :], h_tiles[TOK * g + 2 * half + j // 4][:, j % 4, :], ident_b[:])
                dst = hg[:, 1024 * half : 1024 * (half + 1)].rearrange("p (i k t) -> p i k t", i=2, t=4)
                src = ht[:].rearrange("p (i t) k -> p i k t", t=4)
                if half == 0:
                    nc.scalar.copy(out=dst, in_=src)
                else:
                    nc.vector.tensor_copy(out=dst, in_=src)

        def quantise(g):
            nc.vector.quantize_mx(out=hq[g][:].bitcast(FP8X4), scales=hs[g][:], in_=hg_tiles[g][:])

        for u in range(TOK):
            open_unit(u)
        for which in range(2):
            for kg in range(KX):
                for u in range(TOK):
                    stage1_pass(u, which, kg)
            for u in range(TOK):
                if which == 0:
                    silu(u)
                else:
                    gate(u)
        early = range(TOK, TOK + 3)
        for u in early:
            open_unit(u)
        for which in range(2):
            for u in early:
                for kg in range(KX):
                    stage1_pass(u, which, kg)
                if which == 0:
                    silu(u)
                else:
                    gate(u)
        transposes(0)
        for u in range(TOK + 3, TOK * KH):
            open_unit(u)
            for which in range(2):
                for kg in range(KX):
                    stage1_pass(u, which, kg)
            silu(u)
            gate(u)
            if u == TOK + 3:
                quantise(0)
            if u % TOK == 1:
                transposes(u // TOK - 1)
            if u % TOK == 2:
                quantise(u // TOK - 1)

        def down_pass(acc, i, c0, width, g):
            nc.tensor.matmul_mx(
                out=acc[:],
                lhsT=hq[g][:, P * i : P * (i + 1)].bitcast(FP8X4),
                lhsT_scale=hs[g][:, P * i : P * (i + 1)],
                rhs=dw[g][:, c0 : c0 + width].bitcast(FP8X4),
                rhs_scale=s2[4 * (g % 4) : P, g // 4, c0 : c0 + width],
                start=(g == 0),
                stop=(g == KH - 1),
            )

        def evacuate(acc, i, c0, width, on_vector):
            o = work.tile([P, width], F32, name="o", tag="o", bufs=9)
            if on_vector:
                nc.vector.tensor_copy(out=o[:], in_=acc[:])
            else:
                nc.scalar.copy(out=o[:], in_=acc[:])
            nc.sync.dma_start(out=out[P * i : P * (i + 1), c0 : c0 + width], in_=o[:])

        acc0 = [bank(0 + dc, [P, N], F32, "acc0") for dc in range(DC)]
        acc1 = [bank(2 + dc, [P, N], F32, "acc1") for dc in range(DC)]
        for g in range(KH - 1):
            if g == (KH - 1) // 2:
                transposes(KH - 1)
                quantise(KH - 1)
            for i, pair_accs in ((0, acc0), (1, acc1)):
                for dc in range(DC):
                    down_pass(pair_accs[dc], i, N * dc, N, g)
        for i, pair_accs in ((0, acc0), (1, acc1)):
            for dc in range(DC):
                down_pass(pair_accs[dc], i, N * dc, N, KH - 1)
                evacuate(pair_accs[dc], i, N * dc, N, dc == 0)
        last = (
            (2, 4, 0, N, True),
            (2, 5, N, N, False),
            (3, 6, 0, N, True),
            (3, 7, N, N // 2, False),
            (3, 0, N + N // 2, N // 2, True),
        )
        for i, b, c0, width, on_vector in last:
            acc = bank(b, [P, width], F32, "acc")
            for g in range(KH):
                down_pass(acc, i, c0, width, g)
            evacuate(acc, i, c0, width, on_vector)
